import numpy as np
import ml_dtypes

BF16 = ml_dtypes.bfloat16


def bf(x):
    return np.asarray(x, np.float32).astype(BF16)


def f32(x):
    return np.asarray(x, np.float32)


def f64(x):
    return np.asarray(x).astype(np.float64)


def striped(idx):
    return np.tile(idx.reshape(-1, 16).T, (8, 1))


C, D, S, N = 128, 64, 2048, 256
BASE, FACTOR, LOW, HIGH = 10000.0, 40.0, 10, 23


def yarn_cache():
    ar = np.arange(0, D, 2, dtype=np.float32) / D
    freq_extra = 1.0 / BASE ** ar
    freq_inter = 1.0 / (FACTOR * BASE ** ar)
    ramp = np.clip((np.arange(D // 2, dtype=np.float32) - LOW) / (HIGH - LOW), 0.0, 1.0)
    mask = 1.0 - ramp
    inv_freq = freq_inter * (1 - mask) + freq_extra * mask
    freqs = np.outer(np.arange(S, dtype=np.float32), inv_freq)
    emb = np.concatenate([freqs, freqs], axis=-1)
    return np.concatenate([np.cos(emb).T, np.sin(emb).T], axis=0)


def setup_inputs():
    return {"cs": f32(yarn_cache()), "qk": f32(np.random.standard_normal((C, N))), "offs": striped(np.random.permutation(S)[:N])}


def reference(cs, qk, offs):
    idx = offs[:16].T.reshape(-1)
    t = f64(cs)[:, idx]
    cos, sin = t[:D], t[D:]
    x = f64(qk).reshape(C // D, D // 2, 2, N)
    x1, x2 = x[:, :, 0], x[:, :, 1]
    u = np.concatenate([x1, x2], axis=1)
    v = np.concatenate([-x2, x1], axis=1)
    return (cos[None] * u + sin[None] * v).reshape(C, N)

@@ -1,0 +1,64 @@
+import concourse.mybir as mybir
+
+F32 = mybir.dt.float32
+U16 = mybir.dt.uint16
+MULT = mybir.AluOpType.mult
+ADD = mybir.AluOpType.add
+NOT_EQUAL = mybir.AluOpType.not_equal
+
+P = 128
+S = 2048
+N = 256
+D = 64
+PAIRS = D // 2
+
+FLOPS = 3 * P * N
+
+
+def tile_deepseekv2litedecoderlayer_kernel(tc, cs, qk, offs, out):
+    nc = tc.nc
+    pairs = qk.rearrange("(h i parity) j -> parity h i j", h=2, parity=2)
+    even, odd = pairs[0], pairs[1]
+
+    with tc.tile_pool(name="held", bufs=1) as held, tc.psum_pool(name="psum", bufs=1) as psum:
+        offsets = held.tile([P, N // 16], U16, name="offsets")
+        nc.sync.dma_start(offsets[:], offs)
+        table = held.tile([P, S], F32, name="table")
+        nc.sync.dma_start(table[:], cs)
+
+        factor_stays = held.tile([P, N], F32, name="factor_stays")
+        factor_crosses = held.tile([P, N], F32, name="factor_crosses")
+        for factor, queue, h_cos, h_sin in (
+            (factor_crosses, nc.scalar, 1, 0),
+            (factor_stays, nc.gpsimd, 0, 1),
+        ):
+            queue.dma_start(factor[0 * PAIRS : 1 * PAIRS, :], even[h_cos])
+            queue.dma_start(factor[1 * PAIRS : 2 * PAIRS, :], odd[h_cos])
+            queue.dma_start(factor[2 * PAIRS : 3 * PAIRS, :], odd[h_sin])
+            queue.dma_start(factor[3 * PAIRS : 4 * PAIRS, :], even[h_sin])
+            negated = factor[2 * PAIRS : 3 * PAIRS, :]
+            nc.vector.tensor_scalar_mul(negated, negated, -1.0)
+
+        swap = held.tile([P, P], F32, name="swap")
+        nc.gpsimd.memset(swap[:], 0.0)
+        nc.gpsimd.affine_select(
+            out=swap[:],
+            in_=swap[:],
+            compare_op=NOT_EQUAL,
+            fill=1.0,
+            base=-D,
+            pattern=[[D, 2], [-1, D]],
+            channel_multiplier=1,
+        )
+
+        crosses = held.tile([P, N], F32, name="crosses")
+        nc.vector.tensor_tensor(crosses[:], table[:].indirect(offsets[:]), factor_crosses[:], MULT)
+        stays = held.tile([P, N], F32, name="stays")
+        nc.vector.tensor_tensor(stays[:], table[:].indirect(offsets[:]), factor_stays[:], MULT)
+
+        crossed = psum.tile([P, N], F32, name="crossed")
+        nc.tensor.matmul(crossed[:], swap[:], crosses[:], start=True, stop=True)
+
+        rotated = held.tile([P, N], F32, name="rotated")
+        nc.vector.tensor_tensor(rotated[:], stays[:], crossed[:], ADD)
+        nc.sync.dma_start(out, rotated[:])

@@ -21,24 +21,6 @@ def tile_deepseekv2litedecoderlayer_kernel(tc, cs, qk, offs, out):
     even, odd = pairs[0], pairs[1]
 
     with tc.tile_pool(name="held", bufs=1) as held, tc.psum_pool(name="psum", bufs=1) as psum:
-        offsets = held.tile([P, N // 16], U16, name="offsets")
-        nc.sync.dma_start(offsets[:], offs)
-        table = held.tile([P, S], F32, name="table")
-        nc.sync.dma_start(table[:], cs)
-
-        factor_stays = held.tile([P, N], F32, name="factor_stays")
-        factor_crosses = held.tile([P, N], F32, name="factor_crosses")
-        for factor, queue, h_cos, h_sin in (
-            (factor_crosses, nc.scalar, 1, 0),
-            (factor_stays, nc.gpsimd, 0, 1),
-        ):
-            queue.dma_start(factor[0 * PAIRS : 1 * PAIRS, :], even[h_cos])
-            queue.dma_start(factor[1 * PAIRS : 2 * PAIRS, :], odd[h_cos])
-            queue.dma_start(factor[2 * PAIRS : 3 * PAIRS, :], odd[h_sin])
-            queue.dma_start(factor[3 * PAIRS : 4 * PAIRS, :], even[h_sin])
-            negated = factor[2 * PAIRS : 3 * PAIRS, :]
-            nc.vector.tensor_scalar_mul(negated, negated, -1.0)
-
         swap = held.tile([P, P], F32, name="swap")
         nc.gpsimd.memset(swap[:], 0.0)
         nc.gpsimd.affine_select(
@@ -50,6 +32,24 @@ def tile_deepseekv2litedecoderlayer_kernel(tc, cs, qk, offs, out):
             pattern=[[D, 2], [-1, D]],
             channel_multiplier=1,
         )
+
+        offsets = held.tile([P, N // 16], U16, name="offsets")
+        nc.sync.dma_start(offsets[:], offs)
+        table = held.tile([P, S], F32, name="table")
+        nc.sync.dma_start(table[:], cs)
+
+        factor_stays = held.tile([P, N], F32, name="factor_stays")
+        factor_crosses = held.tile([P, N], F32, name="factor_crosses")
+        for factor, queue, h_cos, h_sin in (
+            (factor_crosses, nc.scalar, 1, 0),
+            (factor_stays, nc.sync, 0, 1),
+        ):
+            queue.dma_start(factor[0 * PAIRS : 1 * PAIRS, :], even[h_cos])
+            queue.dma_start(factor[1 * PAIRS : 2 * PAIRS, :], odd[h_cos])
+            queue.dma_start(factor[2 * PAIRS : 3 * PAIRS, :], odd[h_sin])
+            queue.dma_start(factor[3 * PAIRS : 4 * PAIRS, :], even[h_sin])
+            negated = factor[2 * PAIRS : 3 * PAIRS, :]
+            nc.vector.tensor_scalar_mul(negated, negated, -1.0)
 
         crosses = held.tile([P, N], F32, name="crosses")
         nc.vector.tensor_tensor(crosses[:], table[:].indirect(offsets[:]), factor_crosses[:], MULT)

@@ -11,6 +11,8 @@ S = 2048
 N = 256
 D = 64
 PAIRS = D // 2
+PIECES = 2
+WIDTH = N // PIECES
 
 FLOPS = 3 * P * N
 
@@ -52,13 +54,18 @@ def tile_deepseekv2litedecoderlayer_kernel(tc, cs, qk, offs, out):
             nc.vector.tensor_scalar_mul(negated, negated, -1.0)
 
         crosses = held.tile([P, N], F32, name="crosses")
-        nc.vector.tensor_tensor(crosses[:], table[:].indirect(offsets[:]), factor_crosses[:], MULT)
+        crossed = [psum.tile([P, WIDTH], F32, name=f"crossed{k}") for k in range(PIECES)]
+        for k in range(PIECES):
+            tokens = slice(k * WIDTH, (k + 1) * WIDTH)
+            piece = offsets[:, k * WIDTH // 16 : (k + 1) * WIDTH // 16]
+            nc.vector.tensor_tensor(crosses[:, tokens], table[:].indirect(piece), factor_crosses[:, tokens], MULT)
+            nc.tensor.matmul(crossed[k][:], swap[:], crosses[:, tokens], start=True, stop=True)
+
         stays = held.tile([P, N], F32, name="stays")
         nc.vector.tensor_tensor(stays[:], table[:].indirect(offsets[:]), factor_stays[:], MULT)
 
-        crossed = psum.tile([P, N], F32, name="crossed")
-        nc.tensor.matmul(crossed[:], swap[:], crosses[:], start=True, stop=True)
-
         rotated = held.tile([P, N], F32, name="rotated")
-        nc.vector.tensor_tensor(rotated[:], stays[:], crossed[:], ADD)
+        for k in range(PIECES):
+            tokens = slice(k * WIDTH, (k + 1) * WIDTH)
+            nc.vector.tensor_tensor(rotated[:, tokens], stays[:, tokens], crossed[k][:], ADD)
         nc.sync.dma_start(out, rotated[:])

@@ -42,16 +42,16 @@ def tile_deepseekv2litedecoderlayer_kernel(tc, cs, qk, offs, out):
 
         factor_stays = held.tile([P, N], F32, name="factor_stays")
         factor_crosses = held.tile([P, N], F32, name="factor_crosses")
-        for factor, queue, h_cos, h_sin in (
-            (factor_crosses, nc.scalar, 1, 0),
-            (factor_stays, nc.sync, 0, 1),
-        ):
+        factors = ((factor_crosses, nc.scalar, 1, 0), (factor_stays, nc.sync, 0, 1))
+
+        for factor, queue, h_cos, h_sin in factors:
+            negated = factor[2 * PAIRS : 3 * PAIRS, :]
+            nc.scalar.dma_start(negated, odd[h_sin])
+            nc.vector.tensor_scalar_mul(negated, negated, -1.0)
+        for factor, queue, h_cos, h_sin in factors:
             queue.dma_start(factor[0 * PAIRS : 1 * PAIRS, :], even[h_cos])
             queue.dma_start(factor[1 * PAIRS : 2 * PAIRS, :], odd[h_cos])
-            queue.dma_start(factor[2 * PAIRS : 3 * PAIRS, :], odd[h_sin])
             queue.dma_start(factor[3 * PAIRS : 4 * PAIRS, :], even[h_sin])
-            negated = factor[2 * PAIRS : 3 * PAIRS, :]
-            nc.vector.tensor_scalar_mul(negated, negated, -1.0)
 
         crosses = held.tile([P, N], F32, name="crosses")
         crossed = [psum.tile([P, WIDTH], F32, name=f"crossed{k}") for k in range(PIECES)]

@@ -17,41 +17,51 @@ WIDTH = N // PIECES
 FLOPS = 3 * P * N
 
 
+def mark(nc, columns, base, pattern):
+    nc.gpsimd.affine_select(
+        out=columns,
+        in_=columns,
+        compare_op=NOT_EQUAL,
+        fill=1.0,
+        base=base,
+        pattern=pattern,
+        channel_multiplier=1,
+    )
+
+
 def tile_deepseekv2litedecoderlayer_kernel(tc, cs, qk, offs, out):
     nc = tc.nc
-    pairs = qk.rearrange("(h i parity) j -> parity h i j", h=2, parity=2)
-    even, odd = pairs[0], pairs[1]
-
     with tc.tile_pool(name="held", bufs=1) as held, tc.psum_pool(name="psum", bufs=1) as psum:
-        swap = held.tile([P, P], F32, name="swap")
-        nc.gpsimd.memset(swap[:], 0.0)
-        nc.gpsimd.affine_select(
-            out=swap[:],
-            in_=swap[:],
-            compare_op=NOT_EQUAL,
-            fill=1.0,
-            base=-D,
-            pattern=[[D, 2], [-1, D]],
-            channel_multiplier=1,
-        )
-
         offsets = held.tile([P, N // 16], U16, name="offsets")
         nc.sync.dma_start(offsets[:], offs)
         table = held.tile([P, S], F32, name="table")
         nc.sync.dma_start(table[:], cs)
 
-        factor_stays = held.tile([P, N], F32, name="factor_stays")
-        factor_crosses = held.tile([P, N], F32, name="factor_crosses")
-        factors = ((factor_crosses, nc.scalar, 1, 0), (factor_stays, nc.sync, 0, 1))
+        rows = held.tile([P, N], F32, name="rows")
+        nc.scalar.dma_start(rows[:], qk)
+        order_crosses = held.tile([P, P], F32, name="order_crosses")
+        order_stays = held.tile([P, P], F32, name="order_stays")
+        for order, h_cos, h_sin in ((order_crosses, 1, 0), (order_stays, 0, 1)):
+            nc.gpsimd.memset(order[:], 0.0)
+            mark(nc, order[:, 0:D], base=-D * h_cos, pattern=[[-1, 2], [-2, PAIRS]])
+            mark(nc, order[:, D:P], base=-D * h_sin - 1, pattern=[[1, 2], [-2, PAIRS]])
+        swap = held.tile([P, P], F32, name="swap")
+        nc.gpsimd.memset(swap[:], 0.0)
+        mark(nc, swap[:], base=-D, pattern=[[D, 2], [-1, D]])
+        sign = held.tile([P, 1], F32, name="sign")
+        nc.vector.memset(sign[:], 1.0)
+        nc.vector.memset(sign[2 * PAIRS : 3 * PAIRS, :], -1.0)
 
-        for factor, queue, h_cos, h_sin in factors:
-            negated = factor[2 * PAIRS : 3 * PAIRS, :]
-            nc.scalar.dma_start(negated, odd[h_sin])
-            nc.vector.tensor_scalar_mul(negated, negated, -1.0)
-        for factor, queue, h_cos, h_sin in factors:
-            queue.dma_start(factor[0 * PAIRS : 1 * PAIRS, :], even[h_cos])
-            queue.dma_start(factor[1 * PAIRS : 2 * PAIRS, :], odd[h_cos])
-            queue.dma_start(factor[3 * PAIRS : 4 * PAIRS, :], even[h_sin])
+        ordered_crosses = psum.tile([P, N], F32, name="ordered_crosses")
+        nc.tensor.matmul(ordered_crosses[:], order_crosses[:], rows[:], start=True, stop=True)
+        factor_crosses = held.tile([P, N], F32, name="factor_crosses")
+        nc.vector.tensor_scalar_mul(factor_crosses[:], ordered_crosses[:], sign[:])
+        factor_stays = held.tile([P, N], F32, name="factor_stays")
+        for k in range(PIECES):
+            tokens = slice(k * WIDTH, (k + 1) * WIDTH)
+            ordered_stays = psum.tile([P, WIDTH], F32, name=f"ordered_stays{k}")
+            nc.tensor.matmul(ordered_stays[:], order_stays[:], rows[:, tokens], start=True, stop=True)
+            nc.scalar.mul(factor_stays[:, tokens], ordered_stays[:], sign[:])
 
         crosses = held.tile([P, N], F32, name="crosses")
         crossed = [psum.tile([P, WIDTH], F32, name=f"crossed{k}") for k in range(PIECES)]
@@ -62,7 +72,10 @@ def tile_deepseekv2litedecoderlayer_kernel(tc, cs, qk, offs, out):
             nc.tensor.matmul(crossed[k][:], swap[:], crosses[:, tokens], start=True, stop=True)
 
         stays = held.tile([P, N], F32, name="stays")
-        nc.vector.tensor_tensor(stays[:], table[:].indirect(offsets[:]), factor_stays[:], MULT)
+        for k in range(PIECES):
+            tokens = slice(k * WIDTH, (k + 1) * WIDTH)
+            piece = offsets[:, k * WIDTH // 16 : (k + 1) * WIDTH // 16]
+            nc.vector.tensor_tensor(stays[:, tokens], table[:].indirect(piece), factor_stays[:, tokens], MULT)
 
         rotated = held.tile([P, N], F32, name="rotated")
         for k in range(PIECES):

@@ -32,13 +32,13 @@ def mark(nc, columns, base, pattern):
 def tile_deepseekv2litedecoderlayer_kernel(tc, cs, qk, offs, out):
     nc = tc.nc
     with tc.tile_pool(name="held", bufs=1) as held, tc.psum_pool(name="psum", bufs=1) as psum:
+        rows = held.tile([P, N], F32, name="rows")
+        nc.sync.dma_start(rows[:], qk)
         offsets = held.tile([P, N // 16], U16, name="offsets")
         nc.sync.dma_start(offsets[:], offs)
         table = held.tile([P, S], F32, name="table")
         nc.sync.dma_start(table[:], cs)
 
-        rows = held.tile([P, N], F32, name="rows")
-        nc.scalar.dma_start(rows[:], qk)
         order_crosses = held.tile([P, P], F32, name="order_crosses")
         order_stays = held.tile([P, P], F32, name="order_stays")
         for order, h_cos, h_sin in ((order_crosses, 1, 0), (order_stays, 0, 1)):

@@ -52,10 +52,12 @@ def tile_deepseekv2litedecoderlayer_kernel(tc, cs, qk, offs, out):
         nc.vector.memset(sign[:], 1.0)
         nc.vector.memset(sign[2 * PAIRS : 3 * PAIRS, :], -1.0)
 
-        ordered_crosses = psum.tile([P, N], F32, name="ordered_crosses")
-        nc.tensor.matmul(ordered_crosses[:], order_crosses[:], rows[:], start=True, stop=True)
         factor_crosses = held.tile([P, N], F32, name="factor_crosses")
-        nc.vector.tensor_scalar_mul(factor_crosses[:], ordered_crosses[:], sign[:])
+        for k in range(PIECES):
+            tokens = slice(k * WIDTH, (k + 1) * WIDTH)
+            ordered_crosses = psum.tile([P, WIDTH], F32, name=f"ordered_crosses{k}")
+            nc.tensor.matmul(ordered_crosses[:], order_crosses[:], rows[:, tokens], start=True, stop=True)
+            nc.vector.tensor_scalar_mul(factor_crosses[:, tokens], ordered_crosses[:], sign[:])
         factor_stays = held.tile([P, N], F32, name="factor_stays")
         for k in range(PIECES):
             tokens = slice(k * WIDTH, (k + 1) * WIDTH)

import concourse.mybir as mybir

F32 = mybir.dt.float32
U16 = mybir.dt.uint16
MULT = mybir.AluOpType.mult
ADD = mybir.AluOpType.add
NOT_EQUAL = mybir.AluOpType.not_equal

P = 128
S = 2048
N = 256
D = 64
PAIRS = D // 2
PIECES = 2
WIDTH = N // PIECES

FLOPS = 3 * P * N


def mark(nc, columns, base, pattern):
    nc.gpsimd.affine_select(
        out=columns,
        in_=columns,
        compare_op=NOT_EQUAL,
        fill=1.0,
        base=base,
        pattern=pattern,
        channel_multiplier=1,
    )


def tile_deepseekv2litedecoderlayer_kernel(tc, cs, qk, offs, out):
    nc = tc.nc
    with tc.tile_pool(name="held", bufs=1) as held, tc.psum_pool(name="psum", bufs=1) as psum:
        rows = held.tile([P, N], F32, name="rows")
        nc.sync.dma_start(rows[:], qk)
        offsets = held.tile([P, N // 16], U16, name="offsets")
        nc.sync.dma_start(offsets[:], offs)
        table = held.tile([P, S], F32, name="table")
        nc.sync.dma_start(table[:], cs)

        order_crosses = held.tile([P, P], F32, name="order_crosses")
        order_stays = held.tile([P, P], F32, name="order_stays")
        for order, h_cos, h_sin in ((order_crosses, 1, 0), (order_stays, 0, 1)):
            nc.gpsimd.memset(order[:], 0.0)
            mark(nc, order[:, 0:D], base=-D * h_cos, pattern=[[-1, 2], [-2, PAIRS]])
            mark(nc, order[:, D:P], base=-D * h_sin - 1, pattern=[[1, 2], [-2, PAIRS]])
        swap = held.tile([P, P], F32, name="swap")
        nc.gpsimd.memset(swap[:], 0.0)
        mark(nc, swap[:], base=-D, pattern=[[D, 2], [-1, D]])
        sign = held.tile([P, 1], F32, name="sign")
        nc.vector.memset(sign[:], 1.0)
        nc.vector.memset(sign[2 * PAIRS : 3 * PAIRS, :], -1.0)

        factor_crosses = held.tile([P, N], F32, name="factor_crosses")
        for k in range(PIECES):
            tokens = slice(k * WIDTH, (k + 1) * WIDTH)
            ordered_crosses = psum.tile([P, WIDTH], F32, name=f"ordered_crosses{k}")
            nc.tensor.matmul(ordered_crosses[:], order_crosses[:], rows[:, tokens], start=True, stop=True)
            nc.vector.tensor_scalar_mul(factor_crosses[:, tokens], ordered_crosses[:], sign[:])
        factor_stays = held.tile([P, N], F32, name="factor_stays")
        for k in range(PIECES):
            tokens = slice(k * WIDTH, (k + 1) * WIDTH)
            ordered_stays = psum.tile([P, WIDTH], F32, name=f"ordered_stays{k}")
            nc.tensor.matmul(ordered_stays[:], order_stays[:], rows[:, tokens], start=True, stop=True)
            nc.scalar.mul(factor_stays[:, tokens], ordered_stays[:], sign[:])

        crosses = held.tile([P, N], F32, name="crosses")
        crossed = [psum.tile([P, WIDTH], F32, name=f"crossed{k}") for k in range(PIECES)]
        for k in range(PIECES):
            tokens = slice(k * WIDTH, (k + 1) * WIDTH)
            piece = offsets[:, k * WIDTH // 16 : (k + 1) * WIDTH // 16]
            nc.vector.tensor_tensor(crosses[:, tokens], table[:].indirect(piece), factor_crosses[:, tokens], MULT)
            nc.tensor.matmul(crossed[k][:], swap[:], crosses[:, tokens], start=True, stop=True)

        stays = held.tile([P, N], F32, name="stays")
        for k in range(PIECES):
            tokens = slice(k * WIDTH, (k + 1) * WIDTH)
            piece = offsets[:, k * WIDTH // 16 : (k + 1) * WIDTH // 16]
            nc.vector.tensor_tensor(stays[:, tokens], table[:].indirect(piece), factor_stays[:, tokens], MULT)

        rotated = held.tile([P, N], F32, name="rotated")
        for k in range(PIECES):
            tokens = slice(k * WIDTH, (k + 1) * WIDTH)
            nc.vector.tensor_tensor(rotated[:, tokens], stays[:, tokens], crossed[k][:], ADD)
        nc.sync.dma_start(out, rotated[:])
